import numpy as np
import ml_dtypes


def mxq(x, axis, fmt="e4m3"):
    dtype, down = {"e4m3": (ml_dtypes.float8_e4m3fn, 7), "e5m2": (ml_dtypes.float8_e5m2, 14)}[fmt]
    v = np.moveaxis(np.asarray(x, np.float32).astype(ml_dtypes.bfloat16).astype(np.float64), axis, -1)
    blocks = v.reshape(v.shape[:-1] + (-1, 32))
    amax = np.abs(blocks).max(-1, keepdims=True)
    byte = np.maximum(np.where(amax > 0, np.frexp(amax)[1] - 1 + 127, 0) - down, 1)
    scale = np.exp2(byte - 127.0)
    codes = (blocks / scale).astype(np.float32).astype(dtype).astype(np.float64)
    return np.moveaxis((codes * scale).reshape(v.shape), -1, axis)


WIDE = False


def mx_kscale(k):
    if not WIDE:
        return np.ones(k)
    levels = np.array([20, -20, 10, -10, 0])
    a = np.random.permutation(np.resize(levels, k // 512 * 4)).reshape(k // 512, 4)
    idx = np.arange(k)
    return np.exp2(a[idx // 512, idx % 128 // 32])


BF16 = ml_dtypes.bfloat16


def bf(x):
    return np.asarray(x, np.float32).astype(BF16)


def f64(x):
    return np.asarray(x).astype(np.float64)


B, T, C, R, H, DN, DR, DV = 2, 256, 1536, 512, 16, 128, 64, 128
DQ = DN + DR
NF = DR // 2
N = B * T


def rotate_half(u):
    u1, u2 = u[..., : u.shape[-1] // 2], u[..., u.shape[-1] // 2 :]
    return np.concatenate([-u2, u1], axis=-1)


def cos_sin(freqs_cis):
    freqs = f64(freqs_cis)
    cos = np.tile(freqs[..., 0][None, :, None, :], (1, 1, 1, DR // NF))
    sin = np.tile(freqs[..., 1][None, :, None, :], (1, 1, 1, DR // NF))
    return cos, sin


def setup_inputs():
    s = mx_kscale(N).reshape(B, T)
    x = np.random.standard_normal((B, T, C)) * s[:, :, None]
    freqs_cis = np.stack([np.random.uniform(size=(T, NF)), np.random.uniform(size=(T, NF))], axis=-1)
    w_q = np.random.standard_normal((C, H * DQ)) / np.sqrt(C)
    g = np.random.standard_normal((B, T, H, DQ)) * np.exp2(np.random.randint(-12, 1, (B, T, 1, 1))) / s[:, :, None, None]
    return {"x": bf(x), "freqs_cis": bf(freqs_cis), "w_q": bf(w_q), "grad_out": bf(g)}


def reference(x, freqs_cis, w_q, grad_out):
    g = f64(grad_out)
    cos, sin = cos_sin(freqs_cis)
    g_nope, g_rope = g[..., :DN], g[..., DN:]
    g_rope = g_rope * cos - rotate_half(g_rope) * sin
    gq = np.concatenate([g_nope, g_rope], axis=-1).reshape(N, H * DQ)
    return mxq(f64(x).reshape(N, C), 0, "e4m3").T @ mxq(gq, 0, "e5m2")

@@ -1,0 +1,178 @@
+from contextlib import ExitStack
+
+import concourse.mybir as mybir
+
+BF16 = mybir.dt.bfloat16
+F32 = mybir.dt.float32
+U32 = mybir.dt.uint32
+U8 = mybir.dt.uint8
+E4M3_X4 = mybir.dt.float8_e4m3fn_x4
+E5M2_X4 = mybir.dt.float8_e5m2_x4
+MULT = mybir.AluOpType.mult
+ADD = mybir.AluOpType.add
+
+P = 128
+PACK = 4
+TOKENS = P * PACK
+POSITIONS = 256
+C = 1536
+HEADS = 16
+DN = 128
+DR = 64
+HALF = DR // 2
+DQ = DN + DR
+COLS = HEADS * DQ
+
+M_TILE = 128
+N_TILE = 512
+M_TILES = C // M_TILE
+X_PIECE = 512
+RUN = 4
+
+CHUNK_TILES = (1, 1, 2, 2)
+STAGE_BUFS = 12
+
+FLOPS = 2 * TOKENS * C * COLS
+BYTES = 2 * TOKENS * C + 2 * TOKENS * COLS + 2 * POSITIONS * DR + 4 * C * COLS
+
+
+def plan_chunks():
+    chunks = []
+    first_tile = 0
+    first_head = 0
+    for tiles in CHUNK_TILES:
+        end_col = (first_tile + tiles) * N_TILE
+        end_head = -(-end_col // DQ)
+        chunks.append((first_tile, tiles, first_head, end_head - first_head))
+        first_tile += tiles
+        first_head = end_head
+    return chunks
+
+
+def build_rotation_table(nc, table, freq):
+    cos = freq[:, :, :, 0].rearrange("p j f -> p f j")
+    sin = freq[:, :, :, 1].rearrange("p j f -> p f j")
+    nc.vector.tensor_copy(out=table[:, 0, 0:HALF, :], in_=cos)
+    nc.vector.tensor_copy(out=table[:, 0, HALF:DR, :], in_=sin)
+    nc.vector.tensor_scalar_mul(out=table[:, 1, 0:HALF, :], in0=sin, scalar1=-1.0)
+    nc.vector.tensor_copy(out=table[:, 1, HALF:DR, :], in_=cos)
+
+
+def rotate_and_regroup(nc, work, table, g_raw, g_grouped, heads):
+    rotated_in = g_raw[:, :, :, DN:DQ].rearrange("p j h r -> p h r j")
+    products = work.tile([P, heads, 2, DR, PACK], F32, tag="products")
+    for a in range(2):
+        nc.vector.tensor_tensor(
+            out=products[:, :, a],
+            in0=rotated_in,
+            in1=table[:, a].unsqueeze(1).to_broadcast([P, heads, DR, PACK]),
+            op=MULT,
+        )
+    nc.vector.tensor_copy(
+        out=g_grouped[:, :, 0:DN, :].rearrange("p h (c i) j -> p h c j i", i=RUN),
+        in_=g_raw[:, :, :, 0:DN].rearrange("p j h (c i) -> p h c j i", i=RUN),
+    )
+    nc.vector.tensor_tensor(
+        out=g_grouped[:, :, DN:DQ, :].rearrange("p h (a f) j -> p h a (f j)", a=2),
+        in0=products[:, :, :, 0:HALF, :].rearrange("p h a f j -> p h a (f j)"),
+        in1=products[:, :, :, HALF:DR, :].rearrange("p h a f j -> p h a (f j)"),
+        op=ADD,
+    )
+
+
+def tile_fa3mlaattention_pb_kernel(tc, x, freqs_cis, w_q, grad_out, out):
+    nc = tc.nc
+    chunks = plan_chunks()
+
+    x_rows = x.rearrange("b (q j) c -> (b q) j c", j=PACK)
+    g_rows = grad_out.rearrange("b (q j) h d -> (b q) j h d", j=PACK)
+    freq_rows = freqs_cis.rearrange("(q j) f k -> q j f k", j=PACK)
+
+    with ExitStack() as ctx:
+        keep = ctx.enter_context(tc.tile_pool(name="keep", bufs=1))
+        work = ctx.enter_context(tc.tile_pool(name="work", bufs=2))
+        stages = ctx.enter_context(tc.tile_pool(name="stages", bufs=STAGE_BUFS))
+        banks = ctx.enter_context(tc.psum_pool(name="banks", bufs=8))
+        ctx.enter_context(tc.manual_schedule())
+
+        freq = keep.tile([P, PACK, HALF, 2], BF16)
+        batch_rows = POSITIONS // PACK
+        for b in range(P // batch_rows):
+            nc.scalar.dma_start(out=freq[b * batch_rows : (b + 1) * batch_rows], in_=freq_rows)
+        x_raw = keep.tile([P, PACK, C], BF16)
+        g_raws = []
+        for index, (first_tile, tiles, first_head, heads) in enumerate(chunks):
+            g_raw = keep.tile([P, PACK, heads, DQ], BF16, name="g_raw%d" % index)
+            nc.sync.dma_start(out=g_raw[:], in_=g_rows[:, :, first_head : first_head + heads, :])
+            g_raws.append(g_raw)
+            if index == 0:
+                nc.sync.dma_start(out=x_raw[:], in_=x_rows)
+
+        table = keep.tile([P, 2, DR, PACK], BF16)
+        build_rotation_table(nc, table, freq)
+
+        g_grouped = keep.tile([P, HEADS, DQ, PACK], BF16, align_bytes=64)
+        g_flat = g_grouped[:].rearrange("p h d j -> p (h d j)")
+        g_codes = keep.tile([P, COLS], U32, align_bytes=64)
+        g_scales = keep.tile([P, COLS], U8, align_bytes=64)
+        x_grouped = keep.tile([P, C, PACK], BF16, align_bytes=64)
+        x_flat = x_grouped[:].rearrange("p c j -> p (c j)")
+        x_codes = keep.tile([P, C], U32, align_bytes=64)
+        x_scales = keep.tile([P, C], U8, align_bytes=64)
+
+        for index, (first_tile, tiles, first_head, heads) in enumerate(chunks):
+            rotate_and_regroup(
+                nc, work, table, g_raws[index],
+                g_grouped[:, first_head : first_head + heads], heads,
+            )
+            if index == 0:
+                for c0 in range(0, C, X_PIECE):
+                    nc.vector.tensor_copy(
+                        out=x_grouped[:, c0 : c0 + X_PIECE, :].rearrange("p (c i) j -> p c j i", i=RUN),
+                        in_=x_raw[:, :, c0 : c0 + X_PIECE].rearrange("p j (c i) -> p c j i", i=RUN),
+                    )
+                    if c0 == 0:
+                        nc.vector.quantize_mx(
+                            out=g_codes[:, 0:N_TILE].bitcast(E5M2_X4),
+                            scales=g_scales[:, 0:N_TILE],
+                            in_=g_flat[:, 0 : PACK * N_TILE],
+                        )
+                    nc.vector.quantize_mx(
+                        out=x_codes[:, c0 : c0 + X_PIECE].bitcast(E4M3_X4),
+                        scales=x_scales[:, c0 : c0 + X_PIECE],
+                        in_=x_flat[:, PACK * c0 : PACK * (c0 + X_PIECE)],
+                    )
+            else:
+                for n in range(first_tile, first_tile + tiles):
+                    nc.vector.quantize_mx(
+                        out=g_codes[:, n * N_TILE : (n + 1) * N_TILE].bitcast(E5M2_X4),
+                        scales=g_scales[:, n * N_TILE : (n + 1) * N_TILE],
+                        in_=g_flat[:, PACK * n * N_TILE : PACK * (n + 1) * N_TILE],
+                    )
+
+        for index, (first_tile, tiles, first_head, heads) in enumerate(chunks):
+            vector_helps = index == len(chunks) - 1
+            for m in range(M_TILES):
+                m_cols = slice(m * M_TILE, (m + 1) * M_TILE)
+                stage = stages.tile([P, tiles * N_TILE], F32, tag="stage")
+                for k in range(tiles):
+                    n_cols = slice((first_tile + k) * N_TILE, (first_tile + k + 1) * N_TILE)
+                    bank = banks.tile([P, N_TILE], F32, tag="bank")
+                    nc.tensor.matmul_mx(
+                        out=bank[:],
+                        lhsT=x_codes[:, m_cols].bitcast(E4M3_X4),
+                        lhsT_scale=x_scales[:, m_cols],
+                        rhs=g_codes[:, n_cols].bitcast(E5M2_X4),
+                        rhs_scale=g_scales[:, n_cols],
+                        start=True,
+                        stop=True,
+                    )
+                    stage_cols = slice(k * N_TILE, (k + 1) * N_TILE)
+                    if vector_helps and k % 2 == 1:
+                        nc.vector.tensor_copy(out=stage[:, stage_cols], in_=bank[:])
+                    else:
+                        nc.scalar.copy(out=stage[:, stage_cols], in_=bank[:])
+                nc.sync.dma_start(
+                    out=out[m_cols, first_tile * N_TILE : (first_tile + tiles) * N_TILE],
+                    in_=stage[:],
+                )

@@ -29,8 +29,9 @@ M_TILES = C // M_TILE
 X_PIECE = 512
 RUN = 4
 
-CHUNK_TILES = (1, 1, 2, 2)
+CHUNK_TILES = (1, 2, 3)
 STAGE_BUFS = 12
+SCALAR_REGROUPS_CHUNKS = 2
 
 FLOPS = 2 * TOKENS * C * COLS
 BYTES = 2 * TOKENS * C + 2 * TOKENS * COLS + 2 * POSITIONS * DR + 4 * C * COLS
@@ -58,7 +59,14 @@ def build_rotation_table(nc, table, freq):
     nc.vector.tensor_copy(out=table[:, 1, HALF:DR, :], in_=cos)
 
 
-def rotate_and_regroup(nc, work, table, g_raw, g_grouped, heads):
+def regroup(copy, grouped, raw):
+    copy(
+        out=grouped.rearrange("p (c i) j -> p c j i", i=RUN),
+        in_=raw.rearrange("p j (c i) -> p c j i", i=RUN),
+    )
+
+
+def rotate_and_regroup(nc, work, table, g_raw, g_grouped, heads, scalar_is_idle):
     rotated_in = g_raw[:, :, :, DN:DQ].rearrange("p j h r -> p h r j")
     products = work.tile([P, heads, 2, DR, PACK], F32, tag="products")
     for a in range(2):
@@ -68,10 +76,14 @@ def rotate_and_regroup(nc, work, table, g_raw, g_grouped, heads):
             in1=table[:, a].unsqueeze(1).to_broadcast([P, heads, DR, PACK]),
             op=MULT,
         )
-    nc.vector.tensor_copy(
-        out=g_grouped[:, :, 0:DN, :].rearrange("p h (c i) j -> p h c j i", i=RUN),
-        in_=g_raw[:, :, :, 0:DN].rearrange("p j h (c i) -> p h c j i", i=RUN),
-    )
+    if scalar_is_idle:
+        for h in range(heads):
+            regroup(nc.scalar.copy, g_grouped[:, h, 0:DN, :], g_raw[:, :, h, 0:DN])
+    else:
+        nc.vector.tensor_copy(
+            out=g_grouped[:, :, 0:DN, :].rearrange("p h (c i) j -> p h c j i", i=RUN),
+            in_=g_raw[:, :, :, 0:DN].rearrange("p j h (c i) -> p h c j i", i=RUN),
+        )
     nc.vector.tensor_tensor(
         out=g_grouped[:, :, DN:DQ, :].rearrange("p h (a f) j -> p h a (f j)", a=2),
         in0=products[:, :, :, 0:HALF, :].rearrange("p h a f j -> p h a (f j)"),
@@ -98,7 +110,7 @@ def tile_fa3mlaattention_pb_kernel(tc, x, freqs_cis, w_q, grad_out, out):
         freq = keep.tile([P, PACK, HALF, 2], BF16)
         batch_rows = POSITIONS // PACK
         for b in range(P // batch_rows):
-            nc.scalar.dma_start(out=freq[b * batch_rows : (b + 1) * batch_rows], in_=freq_rows)
+            nc.sync.dma_start(out=freq[b * batch_rows : (b + 1) * batch_rows], in_=freq_rows)
         x_raw = keep.tile([P, PACK, C], BF16)
         g_raws = []
         for index, (first_tile, tiles, first_head, heads) in enumerate(chunks):
@@ -124,30 +136,22 @@ def tile_fa3mlaattention_pb_kernel(tc, x, freqs_cis, w_q, grad_out, out):
             rotate_and_regroup(
                 nc, work, table, g_raws[index],
                 g_grouped[:, first_head : first_head + heads], heads,
+                scalar_is_idle=(index < SCALAR_REGROUPS_CHUNKS),
             )
+            for n in range(first_tile, first_tile + tiles):
+                nc.vector.quantize_mx(
+                    out=g_codes[:, n * N_TILE : (n + 1) * N_TILE].bitcast(E5M2_X4),
+                    scales=g_scales[:, n * N_TILE : (n + 1) * N_TILE],
+                    in_=g_flat[:, PACK * n * N_TILE : PACK * (n + 1) * N_TILE],
+                )
             if index == 0:
                 for c0 in range(0, C, X_PIECE):
-                    nc.vector.tensor_copy(
-                        out=x_grouped[:, c0 : c0 + X_PIECE, :].rearrange("p (c i) j -> p c j i", i=RUN),
-                        in_=x_raw[:, :, c0 : c0 + X_PIECE].rearrange("p j (c i) -> p c j i", i=RUN),
-                    )
-                    if c0 == 0:
-                        nc.vector.quantize_mx(
-                            out=g_codes[:, 0:N_TILE].bitcast(E5M2_X4),
-                            scales=g_scales[:, 0:N_TILE],
-                            in_=g_flat[:, 0 : PACK * N_TILE],
-                        )
+                    copy = nc.scalar.copy if c0 == C - X_PIECE else nc.vector.tensor_copy
+                    regroup(copy, x_grouped[:, c0 : c0 + X_PIECE, :], x_raw[:, :, c0 : c0 + X_PIECE])
                     nc.vector.quantize_mx(
                         out=x_codes[:, c0 : c0 + X_PIECE].bitcast(E4M3_X4),
                         scales=x_scales[:, c0 : c0 + X_PIECE],
                         in_=x_flat[:, PACK * c0 : PACK * (c0 + X_PIECE)],
-                    )
-            else:
-                for n in range(first_tile, first_tile + tiles):
-                    nc.vector.quantize_mx(
-                        out=g_codes[:, n * N_TILE : (n + 1) * N_TILE].bitcast(E5M2_X4),
-                        scales=g_scales[:, n * N_TILE : (n + 1) * N_TILE],
-                        in_=g_flat[:, PACK * n * N_TILE : PACK * (n + 1) * N_TILE],
                     )
 
         for index, (first_tile, tiles, first_head, heads) in enumerate(chunks):

@@ -67,12 +67,16 @@ def regroup(copy, grouped, raw):
 
 
 def rotate_and_regroup(nc, work, table, g_raw, g_grouped, heads, scalar_is_idle):
-    rotated_in = g_raw[:, :, :, DN:DQ].rearrange("p j h r -> p h r j")
+    rotated = g_grouped[:, :, DN:DQ, :]
+    nc.vector.tensor_copy(
+        out=rotated.rearrange("p h (c i) j -> p h c j i", i=RUN),
+        in_=g_raw[:, :, :, DN:DQ].rearrange("p j h (c i) -> p h c j i", i=RUN),
+    )
     products = work.tile([P, heads, 2, DR, PACK], F32, tag="products")
     for a in range(2):
         nc.vector.tensor_tensor(
             out=products[:, :, a],
-            in0=rotated_in,
+            in0=rotated,
             in1=table[:, a].unsqueeze(1).to_broadcast([P, heads, DR, PACK]),
             op=MULT,
         )
@@ -85,7 +89,7 @@ def rotate_and_regroup(nc, work, table, g_raw, g_grouped, heads, scalar_is_idle)
             in_=g_raw[:, :, :, 0:DN].rearrange("p j h (c i) -> p h c j i", i=RUN),
         )
     nc.vector.tensor_tensor(
-        out=g_grouped[:, :, DN:DQ, :].rearrange("p h (a f) j -> p h a (f j)", a=2),
+        out=rotated.rearrange("p h (a f) j -> p h a (f j)", a=2),
         in0=products[:, :, :, 0:HALF, :].rearrange("p h a f j -> p h a (f j)"),
         in1=products[:, :, :, HALF:DR, :].rearrange("p h a f j -> p h a (f j)"),
         op=ADD,

@@ -29,7 +29,7 @@ M_TILES = C // M_TILE
 X_PIECE = 512
 RUN = 4
 
-CHUNK_TILES = (1, 2, 3)
+CHUNK_TILES = (1, 1, 2, 2)
 STAGE_BUFS = 12
 SCALAR_REGROUPS_CHUNKS = 2
 
@@ -67,16 +67,12 @@ def regroup(copy, grouped, raw):
 
 
 def rotate_and_regroup(nc, work, table, g_raw, g_grouped, heads, scalar_is_idle):
-    rotated = g_grouped[:, :, DN:DQ, :]
-    nc.vector.tensor_copy(
-        out=rotated.rearrange("p h (c i) j -> p h c j i", i=RUN),
-        in_=g_raw[:, :, :, DN:DQ].rearrange("p j h (c i) -> p h c j i", i=RUN),
-    )
+    rotated_in = g_raw[:, :, :, DN:DQ].rearrange("p j h r -> p h r j")
     products = work.tile([P, heads, 2, DR, PACK], F32, tag="products")
     for a in range(2):
         nc.vector.tensor_tensor(
             out=products[:, :, a],
-            in0=rotated,
+            in0=rotated_in,
             in1=table[:, a].unsqueeze(1).to_broadcast([P, heads, DR, PACK]),
             op=MULT,
         )
@@ -89,7 +85,7 @@ def rotate_and_regroup(nc, work, table, g_raw, g_grouped, heads, scalar_is_idle)
             in_=g_raw[:, :, :, 0:DN].rearrange("p j h (c i) -> p h c j i", i=RUN),
         )
     nc.vector.tensor_tensor(
-        out=rotated.rearrange("p h (a f) j -> p h a (f j)", a=2),
+        out=g_grouped[:, :, DN:DQ, :].rearrange("p h (a f) j -> p h a (f j)", a=2),
         in0=products[:, :, :, 0:HALF, :].rearrange("p h a f j -> p h a (f j)"),
         in1=products[:, :, :, HALF:DR, :].rearrange("p h a f j -> p h a (f j)"),
         op=ADD,

@@ -31,7 +31,6 @@ RUN = 4
 
 CHUNK_TILES = (1, 1, 2, 2)
 STAGE_BUFS = 12
-SCALAR_REGROUPS_CHUNKS = 2
 
 FLOPS = 2 * TOKENS * C * COLS
 BYTES = 2 * TOKENS * C + 2 * TOKENS * COLS + 2 * POSITIONS * DR + 4 * C * COLS
@@ -40,13 +39,20 @@ BYTES = 2 * TOKENS * C + 2 * TOKENS * COLS + 2 * POSITIONS * DR + 4 * C * COLS
 def plan_chunks():
     chunks = []
     first_tile = 0
-    first_head = 0
     for tiles in CHUNK_TILES:
-        end_col = (first_tile + tiles) * N_TILE
-        end_head = -(-end_col // DQ)
-        chunks.append((first_tile, tiles, first_head, end_head - first_head))
+        begin = first_tile * N_TILE
+        end = begin + tiles * N_TILE
+        rotated = []
+        plain = []
+        for h in range(HEADS):
+            if begin <= h * DQ + DN < end:
+                rotated.append(h)
+            d0 = max(begin - h * DQ, 0)
+            d1 = min(end - h * DQ, DN)
+            if d0 < d1:
+                plain.append((h, d0, d1))
+        chunks.append((first_tile, tiles, rotated, plain))
         first_tile += tiles
-        first_head = end_head
     return chunks
 
 
@@ -66,26 +72,9 @@ def regroup(copy, grouped, raw):
     )
 
 
-def rotate_and_regroup(nc, work, table, g_raw, g_grouped, heads, scalar_is_idle):
-    rotated_in = g_raw[:, :, :, DN:DQ].rearrange("p j h r -> p h r j")
-    products = work.tile([P, heads, 2, DR, PACK], F32, tag="products")
-    for a in range(2):
-        nc.vector.tensor_tensor(
-            out=products[:, :, a],
-            in0=rotated_in,
-            in1=table[:, a].unsqueeze(1).to_broadcast([P, heads, DR, PACK]),
-            op=MULT,
-        )
-    if scalar_is_idle:
-        for h in range(heads):
-            regroup(nc.scalar.copy, g_grouped[:, h, 0:DN, :], g_raw[:, :, h, 0:DN])
-    else:
-        nc.vector.tensor_copy(
-            out=g_grouped[:, :, 0:DN, :].rearrange("p h (c i) j -> p h c j i", i=RUN),
-            in_=g_raw[:, :, :, 0:DN].rearrange("p j h (c i) -> p h c j i", i=RUN),
-        )
+def add_products(nc, products, rotated_out):
     nc.vector.tensor_tensor(
-        out=g_grouped[:, :, DN:DQ, :].rearrange("p h (a f) j -> p h a (f j)", a=2),
+        out=rotated_out.rearrange("p h (a f) j -> p h a (f j)", a=2),
         in0=products[:, :, :, 0:HALF, :].rearrange("p h a f j -> p h a (f j)"),
         in1=products[:, :, :, HALF:DR, :].rearrange("p h a f j -> p h a (f j)"),
         op=ADD,
@@ -97,7 +86,7 @@ def tile_fa3mlaattention_pb_kernel(tc, x, freqs_cis, w_q, grad_out, out):
     chunks = plan_chunks()
 
     x_rows = x.rearrange("b (q j) c -> (b q) j c", j=PACK)
-    g_rows = grad_out.rearrange("b (q j) h d -> (b q) j h d", j=PACK)
+    g_rows = grad_out.rearrange("b (q j) h d -> (b q) j (h d)", j=PACK)
     freq_rows = freqs_cis.rearrange("(q j) f k -> q j f k", j=PACK)
 
     with ExitStack() as ctx:
@@ -111,14 +100,19 @@ def tile_fa3mlaattention_pb_kernel(tc, x, freqs_cis, w_q, grad_out, out):
         batch_rows = POSITIONS // PACK
         for b in range(P // batch_rows):
             nc.sync.dma_start(out=freq[b * batch_rows : (b + 1) * batch_rows], in_=freq_rows)
-        x_raw = keep.tile([P, PACK, C], BF16)
+        x_first = keep.tile([P, PACK, X_PIECE], BF16)
+        x_rest = keep.tile([P, PACK, C - X_PIECE], BF16)
         g_raws = []
-        for index, (first_tile, tiles, first_head, heads) in enumerate(chunks):
-            g_raw = keep.tile([P, PACK, heads, DQ], BF16, name="g_raw%d" % index)
-            nc.sync.dma_start(out=g_raw[:], in_=g_rows[:, :, first_head : first_head + heads, :])
+        for index, (first_tile, tiles, rotated, plain) in enumerate(chunks):
+            g_raw = keep.tile([P, PACK, tiles * N_TILE + DQ], BF16, name="g_raw%d" % index)
+            nc.sync.dma_start(
+                out=g_raw[:, :, 0 : tiles * N_TILE],
+                in_=g_rows[:, :, first_tile * N_TILE : (first_tile + tiles) * N_TILE],
+            )
             g_raws.append(g_raw)
             if index == 0:
-                nc.sync.dma_start(out=x_raw[:], in_=x_rows)
+                nc.sync.dma_start(out=x_first[:], in_=x_rows[:, :, 0:X_PIECE])
+                nc.sync.dma_start(out=x_rest[:], in_=x_rows[:, :, X_PIECE:C])
 
         table = keep.tile([P, 2, DR, PACK], BF16)
         build_rotation_table(nc, table, freq)
@@ -132,31 +126,70 @@ def tile_fa3mlaattention_pb_kernel(tc, x, freqs_cis, w_q, grad_out, out):
         x_codes = keep.tile([P, C], U32, align_bytes=64)
         x_scales = keep.tile([P, C], U8, align_bytes=64)
 
-        for index, (first_tile, tiles, first_head, heads) in enumerate(chunks):
-            rotate_and_regroup(
-                nc, work, table, g_raws[index],
-                g_grouped[:, first_head : first_head + heads], heads,
-                scalar_is_idle=(index < SCALAR_REGROUPS_CHUNKS),
-            )
-            for n in range(first_tile, first_tile + tiles):
-                nc.vector.quantize_mx(
-                    out=g_codes[:, n * N_TILE : (n + 1) * N_TILE].bitcast(E5M2_X4),
-                    scales=g_scales[:, n * N_TILE : (n + 1) * N_TILE],
-                    in_=g_flat[:, PACK * n * N_TILE : PACK * (n + 1) * N_TILE],
-                )
-            if index == 0:
-                for c0 in range(0, C, X_PIECE):
-                    copy = nc.scalar.copy if c0 == C - X_PIECE else nc.vector.tensor_copy
-                    regroup(copy, x_grouped[:, c0 : c0 + X_PIECE, :], x_raw[:, :, c0 : c0 + X_PIECE])
-                    nc.vector.quantize_mx(
-                        out=x_codes[:, c0 : c0 + X_PIECE].bitcast(E4M3_X4),
-                        scales=x_scales[:, c0 : c0 + X_PIECE],
-                        in_=x_flat[:, PACK * c0 : PACK * (c0 + X_PIECE)],
-                    )
+        def raw_heads(index, first_head, heads, d0, d1):
+            start = first_head * DQ + d0 - chunks[index][0] * N_TILE
+            by_head = g_raws[index][:, :, start : start + heads * DQ].rearrange("p j (h d) -> p j h d", d=DQ)
+            return by_head[:, :, :, 0 : d1 - d0]
 
-        for index, (first_tile, tiles, first_head, heads) in enumerate(chunks):
+        def multiply(index):
+            rotated = chunks[index][2]
+            heads = len(rotated)
+            rotated_in = raw_heads(index, rotated[0], heads, DN, DQ).rearrange("p j h r -> p h r j")
+            products = work.tile([P, heads, 2, DR, PACK], F32, tag="products")
+            for a in range(2):
+                nc.vector.tensor_tensor(
+                    out=products[:, :, a],
+                    in0=rotated_in,
+                    in1=table[:, a].unsqueeze(1).to_broadcast([P, heads, DR, PACK]),
+                    op=MULT,
+                )
+            return products
+
+        def add(index, products):
+            rotated = chunks[index][2]
+            add_products(nc, products, g_grouped[:, rotated[0] : rotated[0] + len(rotated), DN:DQ, :])
+
+        def regroup_piece(copy, index, piece):
+            h, d0, d1 = chunks[index][3][piece]
+            regroup(copy, g_grouped[:, h, d0:d1, :], raw_heads(index, h, 1, d0, d1)[:, :, 0, :])
+
+        def vector_regroups_plain(index):
+            plain = chunks[index][3]
+            whole = []
+            for piece, (h, d0, d1) in enumerate(plain):
+                if d1 - d0 == DN:
+                    whole.append(h)
+                else:
+                    regroup_piece(nc.vector.tensor_copy, index, piece)
+            nc.vector.tensor_copy(
+                out=g_grouped[:, whole[0] : whole[0] + len(whole), 0:DN, :].rearrange("p h (c i) j -> p h c j i", i=RUN),
+                in_=raw_heads(index, whole[0], len(whole), 0, DN).rearrange("p j h (c i) -> p h c j i", i=RUN),
+            )
+
+        def quantise_g(n):
+            nc.vector.quantize_mx(
+                out=g_codes[:, n * N_TILE : (n + 1) * N_TILE].bitcast(E5M2_X4),
+                scales=g_scales[:, n * N_TILE : (n + 1) * N_TILE],
+                in_=g_flat[:, PACK * n * N_TILE : PACK * (n + 1) * N_TILE],
+            )
+
+        def regroup_x(copy, c0, c1):
+            if c1 <= X_PIECE:
+                regroup(copy, x_grouped[:, c0:c1, :], x_first[:, :, c0:c1])
+            else:
+                regroup(copy, x_grouped[:, c0:c1, :], x_rest[:, :, c0 - X_PIECE : c1 - X_PIECE])
+
+        def quantise_x(c0, c1):
+            nc.vector.quantize_mx(
+                out=x_codes[:, c0:c1].bitcast(E4M3_X4),
+                scales=x_scales[:, c0:c1],
+                in_=x_flat[:, PACK * c0 : PACK * c1],
+            )
+
+        def emit_rows(index, first_m, end_m):
+            first_tile, tiles = chunks[index][0], chunks[index][1]
             vector_helps = index == len(chunks) - 1
-            for m in range(M_TILES):
+            for m in range(first_m, end_m):
                 m_cols = slice(m * M_TILE, (m + 1) * M_TILE)
                 stage = stages.tile([P, tiles * N_TILE], F32, tag="stage")
                 for k in range(tiles):
@@ -180,3 +213,36 @@ def tile_fa3mlaattention_pb_kernel(tc, x, freqs_cis, w_q, grad_out, out):
                     out=out[m_cols, first_tile * N_TILE : (first_tile + tiles) * N_TILE],
                     in_=stage[:],
                 )
+
+        half_piece = X_PIECE // 2
+        products = multiply(0)
+        for piece in range(len(chunks[0][3])):
+            regroup_piece(nc.scalar.copy, 0, piece)
+        regroup_x(nc.scalar.copy, 0, half_piece)
+        regroup_x(nc.scalar.copy, half_piece, X_PIECE)
+        add(0, products)
+        quantise_g(0)
+        quantise_x(0, half_piece)
+        emit_rows(0, 0, 2)
+        regroup_piece(nc.scalar.copy, 1, 0)
+        regroup_x(nc.vector.tensor_copy, X_PIECE, 2 * X_PIECE)
+        quantise_x(half_piece, X_PIECE)
+        emit_rows(0, 2, 4)
+        regroup_piece(nc.scalar.copy, 1, 1)
+        regroup_x(nc.vector.tensor_copy, 2 * X_PIECE, C)
+        quantise_x(X_PIECE, 2 * X_PIECE)
+        emit_rows(0, 4, 6)
+        regroup_piece(nc.scalar.copy, 1, 2)
+        products = multiply(1)
+        quantise_x(2 * X_PIECE, C)
+        add(1, products)
+        quantise_g(1)
+        emit_rows(0, 6, M_TILES)
+        for index in range(2, len(chunks)):
+            products = multiply(index)
+            vector_regroups_plain(index)
+            add(index, products)
+            for n in range(chunks[index][0], chunks[index][0] + chunks[index][1]):
+                quantise_g(n)
+        for index in range(1, len(chunks)):
+            emit_rows(index, 0, M_TILES)

@@ -30,6 +30,7 @@ X_PIECE = 512
 RUN = 4
 
 CHUNK_TILES = (1, 1, 2, 2)
+LOAD_TILES = (1, 1, 4)
 STAGE_BUFS = 12
 
 FLOPS = 2 * TOKENS * C * COLS
@@ -102,14 +103,17 @@ def tile_fa3mlaattention_pb_kernel(tc, x, freqs_cis, w_q, grad_out, out):
             nc.sync.dma_start(out=freq[b * batch_rows : (b + 1) * batch_rows], in_=freq_rows)
         x_first = keep.tile([P, PACK, X_PIECE], BF16)
         x_rest = keep.tile([P, PACK, C - X_PIECE], BF16)
-        g_raws = []
-        for index, (first_tile, tiles, rotated, plain) in enumerate(chunks):
+        raw_of_tile = []
+        first_tile = 0
+        for index, tiles in enumerate(LOAD_TILES):
             g_raw = keep.tile([P, PACK, tiles * N_TILE + DQ], BF16, name="g_raw%d" % index)
             nc.sync.dma_start(
                 out=g_raw[:, :, 0 : tiles * N_TILE],
                 in_=g_rows[:, :, first_tile * N_TILE : (first_tile + tiles) * N_TILE],
             )
-            g_raws.append(g_raw)
+            for n in range(tiles):
+                raw_of_tile.append((g_raw, first_tile * N_TILE))
+            first_tile += tiles
             if index == 0:
                 nc.sync.dma_start(out=x_first[:], in_=x_rows[:, :, 0:X_PIECE])
                 nc.sync.dma_start(out=x_rest[:], in_=x_rows[:, :, X_PIECE:C])
@@ -127,8 +131,9 @@ def tile_fa3mlaattention_pb_kernel(tc, x, freqs_cis, w_q, grad_out, out):
         x_scales = keep.tile([P, C], U8, align_bytes=64)
 
         def raw_heads(index, first_head, heads, d0, d1):
-            start = first_head * DQ + d0 - chunks[index][0] * N_TILE
-            by_head = g_raws[index][:, :, start : start + heads * DQ].rearrange("p j (h d) -> p j h d", d=DQ)
+            g_raw, first_col = raw_of_tile[chunks[index][0]]
+            start = first_head * DQ + d0 - first_col
+            by_head = g_raw[:, :, start : start + heads * DQ].rearrange("p j (h d) -> p j h d", d=DQ)
             return by_head[:, :, :, 0 : d1 - d0]
 
         def multiply(index):
@@ -216,8 +221,9 @@ def tile_fa3mlaattention_pb_kernel(tc, x, freqs_cis, w_q, grad_out, out):
 
         half_piece = X_PIECE // 2
         products = multiply(0)
-        for piece in range(len(chunks[0][3])):
-            regroup_piece(nc.scalar.copy, 0, piece)
+        regroup_piece(nc.scalar.copy, 0, 0)
+        regroup_piece(nc.scalar.copy, 0, 1)
+        regroup_piece(nc.vector.tensor_copy, 0, 2)
         regroup_x(nc.scalar.copy, 0, half_piece)
         regroup_x(nc.scalar.copy, half_piece, X_PIECE)
         add(0, products)
@@ -232,7 +238,7 @@ def tile_fa3mlaattention_pb_kernel(tc, x, freqs_cis, w_q, grad_out, out):
         regroup_x(nc.vector.tensor_copy, 2 * X_PIECE, C)
         quantise_x(X_PIECE, 2 * X_PIECE)
         emit_rows(0, 4, 6)
-        regroup_piece(nc.scalar.copy, 1, 2)
+        regroup_piece(nc.vector.tensor_copy, 1, 2)
         products = multiply(1)
         quantise_x(2 * X_PIECE, C)
         add(1, products)

from contextlib import ExitStack

import concourse.mybir as mybir

BF16 = mybir.dt.bfloat16
F32 = mybir.dt.float32
U32 = mybir.dt.uint32
U8 = mybir.dt.uint8
E4M3_X4 = mybir.dt.float8_e4m3fn_x4
E5M2_X4 = mybir.dt.float8_e5m2_x4
MULT = mybir.AluOpType.mult
ADD = mybir.AluOpType.add

P = 128
PACK = 4
TOKENS = P * PACK
POSITIONS = 256
C = 1536
HEADS = 16
DN = 128
DR = 64
HALF = DR // 2
DQ = DN + DR
COLS = HEADS * DQ

M_TILE = 128
N_TILE = 512
M_TILES = C // M_TILE
X_PIECE = 512
RUN = 4

CHUNK_TILES = (1, 1, 2, 2)
LOAD_TILES = (1, 1, 4)
STAGE_BUFS = 12

FLOPS = 2 * TOKENS * C * COLS
BYTES = 2 * TOKENS * C + 2 * TOKENS * COLS + 2 * POSITIONS * DR + 4 * C * COLS


def plan_chunks():
    chunks = []
    first_tile = 0
    for tiles in CHUNK_TILES:
        begin = first_tile * N_TILE
        end = begin + tiles * N_TILE
        rotated = []
        plain = []
        for h in range(HEADS):
            if begin <= h * DQ + DN < end:
                rotated.append(h)
            d0 = max(begin - h * DQ, 0)
            d1 = min(end - h * DQ, DN)
            if d0 < d1:
                plain.append((h, d0, d1))
        chunks.append((first_tile, tiles, rotated, plain))
        first_tile += tiles
    return chunks


def build_rotation_table(nc, table, freq):
    cos = freq[:, :, :, 0].rearrange("p j f -> p f j")
    sin = freq[:, :, :, 1].rearrange("p j f -> p f j")
    nc.vector.tensor_copy(out=table[:, 0, 0:HALF, :], in_=cos)
    nc.vector.tensor_copy(out=table[:, 0, HALF:DR, :], in_=sin)
    nc.vector.tensor_scalar_mul(out=table[:, 1, 0:HALF, :], in0=sin, scalar1=-1.0)
    nc.vector.tensor_copy(out=table[:, 1, HALF:DR, :], in_=cos)


def regroup(copy, grouped, raw):
    copy(
        out=grouped.rearrange("p (c i) j -> p c j i", i=RUN),
        in_=raw.rearrange("p j (c i) -> p c j i", i=RUN),
    )


def add_products(nc, products, rotated_out):
    nc.vector.tensor_tensor(
        out=rotated_out.rearrange("p h (a f) j -> p h a (f j)", a=2),
        in0=products[:, :, :, 0:HALF, :].rearrange("p h a f j -> p h a (f j)"),
        in1=products[:, :, :, HALF:DR, :].rearrange("p h a f j -> p h a (f j)"),
        op=ADD,
    )


def tile_fa3mlaattention_pb_kernel(tc, x, freqs_cis, w_q, grad_out, out):
    nc = tc.nc
    chunks = plan_chunks()

    x_rows = x.rearrange("b (q j) c -> (b q) j c", j=PACK)
    g_rows = grad_out.rearrange("b (q j) h d -> (b q) j (h d)", j=PACK)
    freq_rows = freqs_cis.rearrange("(q j) f k -> q j f k", j=PACK)

    with ExitStack() as ctx:
        keep = ctx.enter_context(tc.tile_pool(name="keep", bufs=1))
        work = ctx.enter_context(tc.tile_pool(name="work", bufs=2))
        stages = ctx.enter_context(tc.tile_pool(name="stages", bufs=STAGE_BUFS))
        banks = ctx.enter_context(tc.psum_pool(name="banks", bufs=8))
        ctx.enter_context(tc.manual_schedule())

        freq = keep.tile([P, PACK, HALF, 2], BF16)
        batch_rows = POSITIONS // PACK
        for b in range(P // batch_rows):
            nc.sync.dma_start(out=freq[b * batch_rows : (b + 1) * batch_rows], in_=freq_rows)
        x_first = keep.tile([P, PACK, X_PIECE], BF16)
        x_rest = keep.tile([P, PACK, C - X_PIECE], BF16)
        raw_of_tile = []
        first_tile = 0
        for index, tiles in enumerate(LOAD_TILES):
            g_raw = keep.tile([P, PACK, tiles * N_TILE + DQ], BF16, name="g_raw%d" % index)
            nc.sync.dma_start(
                out=g_raw[:, :, 0 : tiles * N_TILE],
                in_=g_rows[:, :, first_tile * N_TILE : (first_tile + tiles) * N_TILE],
            )
            for n in range(tiles):
                raw_of_tile.append((g_raw, first_tile * N_TILE))
            first_tile += tiles
            if index == 0:
                nc.sync.dma_start(out=x_first[:], in_=x_rows[:, :, 0:X_PIECE])
                nc.sync.dma_start(out=x_rest[:], in_=x_rows[:, :, X_PIECE:C])

        table = keep.tile([P, 2, DR, PACK], BF16)
        build_rotation_table(nc, table, freq)

        g_grouped = keep.tile([P, HEADS, DQ, PACK], BF16, align_bytes=64)
        g_flat = g_grouped[:].rearrange("p h d j -> p (h d j)")
        g_codes = keep.tile([P, COLS], U32, align_bytes=64)
        g_scales = keep.tile([P, COLS], U8, align_bytes=64)
        x_grouped = keep.tile([P, C, PACK], BF16, align_bytes=64)
        x_flat = x_grouped[:].rearrange("p c j -> p (c j)")
        x_codes = keep.tile([P, C], U32, align_bytes=64)
        x_scales = keep.tile([P, C], U8, align_bytes=64)

        def raw_heads(index, first_head, heads, d0, d1):
            g_raw, first_col = raw_of_tile[chunks[index][0]]
            start = first_head * DQ + d0 - first_col
            by_head = g_raw[:, :, start : start + heads * DQ].rearrange("p j (h d) -> p j h d", d=DQ)
            return by_head[:, :, :, 0 : d1 - d0]

        def multiply(index):
            rotated = chunks[index][2]
            heads = len(rotated)
            rotated_in = raw_heads(index, rotated[0], heads, DN, DQ).rearrange("p j h r -> p h r j")
            products = work.tile([P, heads, 2, DR, PACK], F32, tag="products")
            for a in range(2):
                nc.vector.tensor_tensor(
                    out=products[:, :, a],
                    in0=rotated_in,
                    in1=table[:, a].unsqueeze(1).to_broadcast([P, heads, DR, PACK]),
                    op=MULT,
                )
            return products

        def add(index, products):
            rotated = chunks[index][2]
            add_products(nc, products, g_grouped[:, rotated[0] : rotated[0] + len(rotated), DN:DQ, :])

        def regroup_piece(copy, index, piece):
            h, d0, d1 = chunks[index][3][piece]
            regroup(copy, g_grouped[:, h, d0:d1, :], raw_heads(index, h, 1, d0, d1)[:, :, 0, :])

        def vector_regroups_plain(index):
            plain = chunks[index][3]
            whole = []
            for piece, (h, d0, d1) in enumerate(plain):
                if d1 - d0 == DN:
                    whole.append(h)
                else:
                    regroup_piece(nc.vector.tensor_copy, index, piece)
            nc.vector.tensor_copy(
                out=g_grouped[:, whole[0] : whole[0] + len(whole), 0:DN, :].rearrange("p h (c i) j -> p h c j i", i=RUN),
                in_=raw_heads(index, whole[0], len(whole), 0, DN).rearrange("p j h (c i) -> p h c j i", i=RUN),
            )

        def quantise_g(n):
            nc.vector.quantize_mx(
                out=g_codes[:, n * N_TILE : (n + 1) * N_TILE].bitcast(E5M2_X4),
                scales=g_scales[:, n * N_TILE : (n + 1) * N_TILE],
                in_=g_flat[:, PACK * n * N_TILE : PACK * (n + 1) * N_TILE],
            )

        def regroup_x(copy, c0, c1):
            if c1 <= X_PIECE:
                regroup(copy, x_grouped[:, c0:c1, :], x_first[:, :, c0:c1])
            else:
                regroup(copy, x_grouped[:, c0:c1, :], x_rest[:, :, c0 - X_PIECE : c1 - X_PIECE])

        def quantise_x(c0, c1):
            nc.vector.quantize_mx(
                out=x_codes[:, c0:c1].bitcast(E4M3_X4),
                scales=x_scales[:, c0:c1],
                in_=x_flat[:, PACK * c0 : PACK * c1],
            )

        def emit_rows(index, first_m, end_m):
            first_tile, tiles = chunks[index][0], chunks[index][1]
            vector_helps = index == len(chunks) - 1
            for m in range(first_m, end_m):
                m_cols = slice(m * M_TILE, (m + 1) * M_TILE)
                stage = stages.tile([P, tiles * N_TILE], F32, tag="stage")
                for k in range(tiles):
                    n_cols = slice((first_tile + k) * N_TILE, (first_tile + k + 1) * N_TILE)
                    bank = banks.tile([P, N_TILE], F32, tag="bank")
                    nc.tensor.matmul_mx(
                        out=bank[:],
                        lhsT=x_codes[:, m_cols].bitcast(E4M3_X4),
                        lhsT_scale=x_scales[:, m_cols],
                        rhs=g_codes[:, n_cols].bitcast(E5M2_X4),
                        rhs_scale=g_scales[:, n_cols],
                        start=True,
                        stop=True,
                    )
                    stage_cols = slice(k * N_TILE, (k + 1) * N_TILE)
                    if vector_helps and k % 2 == 1:
                        nc.vector.tensor_copy(out=stage[:, stage_cols], in_=bank[:])
                    else:
                        nc.scalar.copy(out=stage[:, stage_cols], in_=bank[:])
                nc.sync.dma_start(
                    out=out[m_cols, first_tile * N_TILE : (first_tile + tiles) * N_TILE],
                    in_=stage[:],
                )

        half_piece = X_PIECE // 2
        products = multiply(0)
        regroup_piece(nc.scalar.copy, 0, 0)
        regroup_piece(nc.scalar.copy, 0, 1)
        regroup_piece(nc.vector.tensor_copy, 0, 2)
        regroup_x(nc.scalar.copy, 0, half_piece)
        regroup_x(nc.scalar.copy, half_piece, X_PIECE)
        add(0, products)
        quantise_g(0)
        quantise_x(0, half_piece)
        emit_rows(0, 0, 2)
        regroup_piece(nc.scalar.copy, 1, 0)
        regroup_x(nc.vector.tensor_copy, X_PIECE, 2 * X_PIECE)
        quantise_x(half_piece, X_PIECE)
        emit_rows(0, 2, 4)
        regroup_piece(nc.scalar.copy, 1, 1)
        regroup_x(nc.vector.tensor_copy, 2 * X_PIECE, C)
        quantise_x(X_PIECE, 2 * X_PIECE)
        emit_rows(0, 4, 6)
        regroup_piece(nc.vector.tensor_copy, 1, 2)
        products = multiply(1)
        quantise_x(2 * X_PIECE, C)
        add(1, products)
        quantise_g(1)
        emit_rows(0, 6, M_TILES)
        for index in range(2, len(chunks)):
            products = multiply(index)
            vector_regroups_plain(index)
            add(index, products)
            for n in range(chunks[index][0], chunks[index][0] + chunks[index][1]):
                quantise_g(n)
        for index in range(1, len(chunks)):
            emit_rows(index, 0, M_TILES)
